import numpy as np
import ml_dtypes

BF16 = ml_dtypes.bfloat16


def bf(x):
    return np.asarray(x, np.float32).astype(BF16)


def f32(x):
    return np.asarray(x, np.float32)


def f64(x):
    return np.asarray(x).astype(np.float64)


def striped(idx):
    return np.tile(idx.reshape(-1, 16).T, (8, 1))


H, L, C, S, N, D = 2, 512, 1024, 384, 128, 256
CTX_SCALE = 4.0


def setup_inputs():
    return {"x": f32(np.random.uniform(size=(C, S))), "tail": f32(np.random.uniform(size=(C, N))), "context": bf(CTX_SCALE * np.random.standard_normal((L, D))), "offs": striped(np.random.permutation(np.tile(np.arange(S), 2))[:N])}


def reference(x, tail, context, offs):
    idx = offs[:16].T.reshape(-1)
    prod = f64(x)[:, idx] * f64(tail)
    ctx = prod.reshape(H, L, N).sum(axis=0)
    ctx = ctx / ctx.sum(axis=0, keepdims=True)
    return f64(context).T @ ctx

@@ -1,0 +1,72 @@
+import concourse.mybir as mybir
+
+HEADS, TOKENS, ENTITIES, PAIRS, FEATURES = 2, 512, 384, 128, 256
+P = 128
+TOKEN_BLOCKS = TOKENS // P
+FEATURE_BLOCKS = FEATURES // P
+FLOPS = 2 * TOKENS * FEATURES * PAIRS
+
+F32, BF16, U16 = mybir.dt.float32, mybir.dt.bfloat16, mybir.dt.uint16
+MULT, ADD = mybir.AluOpType.mult, mybir.AluOpType.add
+
+
+def tile_remodel_mention_kernel(tc, x, tail, context, offs, out):
+    nc = tc.nc
+
+    x_blocks = x.rearrange("(h p k) s -> h k p s", h=HEADS, k=TOKEN_BLOCKS)
+    tail_heads = tail.rearrange("(h p k) n -> h p k n", h=HEADS, k=TOKEN_BLOCKS)
+    context_rows = context.rearrange("(p k) d -> p k d", k=TOKEN_BLOCKS)
+    out_blocks = out.rearrange("(b p) n -> b p n", p=P)
+
+    with (
+        tc.tile_pool(name="held", bufs=1) as held,
+        tc.psum_pool(name="psum", bufs=1) as psum,
+    ):
+        offsets = held.tile([P, PAIRS // 16], U16, name="offsets")
+        nc.sync.dma_start(offsets[:], offs)
+
+        queues = (nc.sync, nc.scalar)
+        tail_tiles = []
+        for h in range(HEADS):
+            tail_tile = held.tile([P, TOKEN_BLOCKS, PAIRS], F32, name=f"tail{h}")
+            queues[h].dma_start(tail_tile[:], tail_heads[h])
+            tail_tiles.append(tail_tile)
+        context_tile = held.tile([P, TOKEN_BLOCKS, FEATURES], BF16, name="context_tile")
+        nc.gpsimd.dma_start(context_tile[:], context_rows)
+        windows = {}
+        for k in range(TOKEN_BLOCKS):
+            for h in range(HEADS):
+                window = held.tile([P, ENTITIES], F32, name=f"window{h}{k}")
+                queues[h].dma_start(window[:], x_blocks[h, k])
+                windows[h, k] = window
+
+        ones = held.tile([P, P], F32, name="ones")
+        nc.gpsimd.memset(ones[:], 1.0)
+
+        den_psum = psum.tile([P, PAIRS], F32, name="den_psum")
+        pooled_psum = [psum.tile([P, PAIRS], F32, name=f"pooled_psum{b}") for b in range(FEATURE_BLOCKS)]
+
+        for k in range(TOKEN_BLOCKS):
+            prods = []
+            for h in range(HEADS):
+                prod = held.tile([P, PAIRS], F32, name=f"prod{h}{k}")
+                nc.vector.tensor_tensor(prod[:], windows[h, k][:].indirect(offsets[:]), tail_tiles[h][:, k, :], MULT)
+                nc.tensor.matmul(
+                    den_psum[:], ones[:], prod[:],
+                    start=(k == 0 and h == 0), stop=(k == TOKEN_BLOCKS - 1 and h == HEADS - 1),
+                )
+                prods.append(prod)
+            ctx = held.tile([P, PAIRS], BF16, name=f"ctx{k}")
+            nc.vector.tensor_tensor(ctx[:], prods[0][:], prods[1][:], ADD)
+            for b in range(FEATURE_BLOCKS):
+                nc.tensor.matmul(
+                    pooled_psum[b][:], context_tile[:, k, b * P : (b + 1) * P], ctx[:],
+                    start=(k == 0), stop=(k == TOKEN_BLOCKS - 1),
+                )
+
+        inverse_den = held.tile([P, PAIRS], F32, name="inverse_den")
+        nc.vector.reciprocal(inverse_den[:], den_psum[:])
+        for b in range(FEATURE_BLOCKS):
+            pooled = held.tile([P, PAIRS], F32, name=f"pooled{b}")
+            nc.vector.tensor_tensor(pooled[:], pooled_psum[b][:], inverse_den[:], MULT)
+            queues[b].dma_start(out_blocks[b], pooled[:])

@@ -1,4 +1,5 @@
 import concourse.mybir as mybir
+from concourse.masks import make_identity
 
 HEADS, TOKENS, ENTITIES, PAIRS, FEATURES = 2, 512, 384, 128, 256
 P = 128
@@ -24,49 +25,61 @@ def tile_remodel_mention_kernel(tc, x, tail, context, offs, out):
     ):
         offsets = held.tile([P, PAIRS // 16], U16, name="offsets")
         nc.sync.dma_start(offsets[:], offs)
-
-        queues = (nc.sync, nc.scalar)
-        tail_tiles = []
+        tail_tiles, windows = [], {}
         for h in range(HEADS):
             tail_tile = held.tile([P, TOKEN_BLOCKS, PAIRS], F32, name=f"tail{h}")
-            queues[h].dma_start(tail_tile[:], tail_heads[h])
+            nc.sync.dma_start(tail_tile[:], tail_heads[h])
             tail_tiles.append(tail_tile)
-        context_tile = held.tile([P, TOKEN_BLOCKS, FEATURES], BF16, name="context_tile")
-        nc.gpsimd.dma_start(context_tile[:], context_rows)
-        windows = {}
-        for k in range(TOKEN_BLOCKS):
-            for h in range(HEADS):
+            for k in range(TOKEN_BLOCKS):
                 window = held.tile([P, ENTITIES], F32, name=f"window{h}{k}")
-                queues[h].dma_start(window[:], x_blocks[h, k])
+                nc.sync.dma_start(window[:], x_blocks[h, k])
                 windows[h, k] = window
+        context_tile = held.tile([P, TOKEN_BLOCKS, FEATURES], BF16, name="context_tile")
+        nc.sync.dma_start(context_tile[:], context_rows)
 
-        ones = held.tile([P, P], F32, name="ones")
-        nc.gpsimd.memset(ones[:], 1.0)
+        ones_column = held.tile([P, 1], F32, name="ones_column")
+        nc.vector.memset(ones_column[:], 1.0)
+        identity = held.tile([P, P], F32, name="identity")
+        make_identity(nc, identity[:])
 
-        den_psum = psum.tile([P, PAIRS], F32, name="den_psum")
-        pooled_psum = [psum.tile([P, PAIRS], F32, name=f"pooled_psum{b}") for b in range(FEATURE_BLOCKS)]
-
-        for k in range(TOKEN_BLOCKS):
-            prods = []
-            for h in range(HEADS):
+        den_psum = psum.tile([P, 1], F32, name="den_psum")
+        prods = {}
+        for h in range(HEADS):
+            for k in range(TOKEN_BLOCKS):
                 prod = held.tile([P, PAIRS], F32, name=f"prod{h}{k}")
                 nc.vector.tensor_tensor(prod[:], windows[h, k][:].indirect(offsets[:]), tail_tiles[h][:, k, :], MULT)
                 nc.tensor.matmul(
-                    den_psum[:], ones[:], prod[:],
-                    start=(k == 0 and h == 0), stop=(k == TOKEN_BLOCKS - 1 and h == HEADS - 1),
+                    den_psum[:], prod[:], ones_column[:],
+                    start=(h == 0 and k == 0), stop=(h == HEADS - 1 and k == TOKEN_BLOCKS - 1),
                 )
-                prods.append(prod)
+                prods[h, k] = prod
+
+        ctxs = []
+        for k in range(TOKEN_BLOCKS):
             ctx = held.tile([P, PAIRS], BF16, name=f"ctx{k}")
-            nc.vector.tensor_tensor(ctx[:], prods[0][:], prods[1][:], ADD)
-            for b in range(FEATURE_BLOCKS):
+            nc.vector.tensor_tensor(ctx[:], prods[0, k][:], prods[1, k][:], ADD)
+            ctxs.append(ctx)
+
+        inverse_den = held.tile([P, 1], F32, name="inverse_den")
+        nc.vector.reciprocal(inverse_den[:], den_psum[:])
+
+        def pool_features(b):
+            pooled_psum = psum.tile([P, PAIRS], F32, name=f"pooled_psum{b}")
+            for k in range(TOKEN_BLOCKS):
                 nc.tensor.matmul(
-                    pooled_psum[b][:], context_tile[:, k, b * P : (b + 1) * P], ctx[:],
+                    pooled_psum[:], context_tile[:, k, b * P : (b + 1) * P], ctxs[k][:],
                     start=(k == 0), stop=(k == TOKEN_BLOCKS - 1),
                 )
+            return pooled_psum
 
-        inverse_den = held.tile([P, PAIRS], F32, name="inverse_den")
-        nc.vector.reciprocal(inverse_den[:], den_psum[:])
-        for b in range(FEATURE_BLOCKS):
+        pooled_psums = [pool_features(0)]
+        spread_psum = psum.tile([P, PAIRS], F32, name="spread_psum")
+        nc.tensor.transpose(spread_psum[:], inverse_den[:, 0:1].to_broadcast([P, P]), identity[:])
+        pooled_psums.append(pool_features(1))
+
+        spread = held.tile([P, PAIRS], F32, name="spread")
+        nc.vector.tensor_copy(spread[:], spread_psum[:])
+        for b, queue in enumerate((nc.sync, nc.scalar)):
             pooled = held.tile([P, PAIRS], F32, name=f"pooled{b}")
-            nc.vector.tensor_tensor(pooled[:], pooled_psum[b][:], inverse_den[:], MULT)
-            queues[b].dma_start(out_blocks[b], pooled[:])
+            nc.vector.tensor_tensor(pooled[:], pooled_psums[b][:], spread[:], MULT)
+            queue.dma_start(out_blocks[b], pooled[:])

@@ -1,5 +1,4 @@
 import concourse.mybir as mybir
-from concourse.masks import make_identity
 
 HEADS, TOKENS, ENTITIES, PAIRS, FEATURES = 2, 512, 384, 128, 256
 P = 128
@@ -37,19 +36,17 @@ def tile_remodel_mention_kernel(tc, x, tail, context, offs, out):
         context_tile = held.tile([P, TOKEN_BLOCKS, FEATURES], BF16, name="context_tile")
         nc.sync.dma_start(context_tile[:], context_rows)
 
-        ones_column = held.tile([P, 1], F32, name="ones_column")
-        nc.vector.memset(ones_column[:], 1.0)
-        identity = held.tile([P, P], F32, name="identity")
-        make_identity(nc, identity[:])
+        ones = held.tile([P, P], F32, name="ones")
+        nc.vector.memset(ones[:], 1.0)
 
-        den_psum = psum.tile([P, 1], F32, name="den_psum")
+        den_psum = psum.tile([P, PAIRS], F32, name="den_psum")
         prods = {}
         for h in range(HEADS):
             for k in range(TOKEN_BLOCKS):
                 prod = held.tile([P, PAIRS], F32, name=f"prod{h}{k}")
                 nc.vector.tensor_tensor(prod[:], windows[h, k][:].indirect(offsets[:]), tail_tiles[h][:, k, :], MULT)
                 nc.tensor.matmul(
-                    den_psum[:], prod[:], ones_column[:],
+                    den_psum[:], ones[:], prod[:],
                     start=(h == 0 and k == 0), stop=(h == HEADS - 1 and k == TOKEN_BLOCKS - 1),
                 )
                 prods[h, k] = prod
@@ -60,26 +57,16 @@ def tile_remodel_mention_kernel(tc, x, tail, context, offs, out):
             nc.vector.tensor_tensor(ctx[:], prods[0, k][:], prods[1, k][:], ADD)
             ctxs.append(ctx)
 
-        inverse_den = held.tile([P, 1], F32, name="inverse_den")
+        inverse_den = held.tile([P, PAIRS], F32, name="inverse_den")
         nc.vector.reciprocal(inverse_den[:], den_psum[:])
 
-        def pool_features(b):
+        for b, queue in enumerate((nc.sync, nc.scalar)):
             pooled_psum = psum.tile([P, PAIRS], F32, name=f"pooled_psum{b}")
             for k in range(TOKEN_BLOCKS):
                 nc.tensor.matmul(
                     pooled_psum[:], context_tile[:, k, b * P : (b + 1) * P], ctxs[k][:],
                     start=(k == 0), stop=(k == TOKEN_BLOCKS - 1),
                 )
-            return pooled_psum
-
-        pooled_psums = [pool_features(0)]
-        spread_psum = psum.tile([P, PAIRS], F32, name="spread_psum")
-        nc.tensor.transpose(spread_psum[:], inverse_den[:, 0:1].to_broadcast([P, P]), identity[:])
-        pooled_psums.append(pool_features(1))
-
-        spread = held.tile([P, PAIRS], F32, name="spread")
-        nc.vector.tensor_copy(spread[:], spread_psum[:])
-        for b, queue in enumerate((nc.sync, nc.scalar)):
             pooled = held.tile([P, PAIRS], F32, name=f"pooled{b}")
-            nc.vector.tensor_tensor(pooled[:], pooled_psums[b][:], spread[:], MULT)
+            nc.vector.tensor_tensor(pooled[:], pooled_psum[:], inverse_den[:], MULT)
             queue.dma_start(out_blocks[b], pooled[:])

@@ -54,7 +54,7 @@ def tile_remodel_mention_kernel(tc, x, tail, context, offs, out):
         ctxs = []
         for k in range(TOKEN_BLOCKS):
             ctx = held.tile([P, PAIRS], BF16, name=f"ctx{k}")
-            nc.vector.tensor_tensor(ctx[:], prods[0, k][:], prods[1, k][:], ADD)
+            nc.gpsimd.tensor_tensor(ctx[:], prods[0, k][:], prods[1, k][:], ADD)
             ctxs.append(ctx)
 
         inverse_den = held.tile([P, PAIRS], F32, name="inverse_den")

@@ -54,19 +54,22 @@ def tile_remodel_mention_kernel(tc, x, tail, context, offs, out):
         ctxs = []
         for k in range(TOKEN_BLOCKS):
             ctx = held.tile([P, PAIRS], BF16, name=f"ctx{k}")
-            nc.gpsimd.tensor_tensor(ctx[:], prods[0, k][:], prods[1, k][:], ADD)
+            adder = nc.vector if k == TOKEN_BLOCKS - 1 else nc.gpsimd
+            adder.tensor_tensor(ctx[:], prods[0, k][:], prods[1, k][:], ADD)
             ctxs.append(ctx)
 
         inverse_den = held.tile([P, PAIRS], F32, name="inverse_den")
         nc.vector.reciprocal(inverse_den[:], den_psum[:])
 
-        for b, queue in enumerate((nc.sync, nc.scalar)):
-            pooled_psum = psum.tile([P, PAIRS], F32, name=f"pooled_psum{b}")
-            for k in range(TOKEN_BLOCKS):
+        pooled_psums = [psum.tile([P, PAIRS], F32, name=f"pooled_psum{b}") for b in range(FEATURE_BLOCKS)]
+        for k in range(TOKEN_BLOCKS):
+            for b in range(FEATURE_BLOCKS):
                 nc.tensor.matmul(
-                    pooled_psum[:], context_tile[:, k, b * P : (b + 1) * P], ctxs[k][:],
+                    pooled_psums[b][:], context_tile[:, k, b * P : (b + 1) * P], ctxs[k][:],
                     start=(k == 0), stop=(k == TOKEN_BLOCKS - 1),
                 )
+
+        for b, queue in enumerate((nc.sync, nc.scalar)):
             pooled = held.tile([P, PAIRS], F32, name=f"pooled{b}")
-            nc.vector.tensor_tensor(pooled[:], pooled_psum[:], inverse_den[:], MULT)
+            nc.vector.tensor_tensor(pooled[:], pooled_psums[b][:], inverse_den[:], MULT)
             queue.dma_start(out_blocks[b], pooled[:])

@@ -27,14 +27,14 @@ def tile_remodel_mention_kernel(tc, x, tail, context, offs, out):
         tail_tiles, windows = [], {}
         for h in range(HEADS):
             tail_tile = held.tile([P, TOKEN_BLOCKS, PAIRS], F32, name=f"tail{h}")
-            nc.sync.dma_start(tail_tile[:], tail_heads[h])
+            nc.scalar.dma_start(tail_tile[:], tail_heads[h])
             tail_tiles.append(tail_tile)
             for k in range(TOKEN_BLOCKS):
                 window = held.tile([P, ENTITIES], F32, name=f"window{h}{k}")
-                nc.sync.dma_start(window[:], x_blocks[h, k])
+                nc.scalar.dma_start(window[:], x_blocks[h, k])
                 windows[h, k] = window
         context_tile = held.tile([P, TOKEN_BLOCKS, FEATURES], BF16, name="context_tile")
-        nc.sync.dma_start(context_tile[:], context_rows)
+        nc.scalar.dma_start(context_tile[:], context_rows)
 
         ones = held.tile([P, P], F32, name="ones")
         nc.vector.memset(ones[:], 1.0)
@@ -54,22 +54,19 @@ def tile_remodel_mention_kernel(tc, x, tail, context, offs, out):
         ctxs = []
         for k in range(TOKEN_BLOCKS):
             ctx = held.tile([P, PAIRS], BF16, name=f"ctx{k}")
-            adder = nc.vector if k == TOKEN_BLOCKS - 1 else nc.gpsimd
-            adder.tensor_tensor(ctx[:], prods[0, k][:], prods[1, k][:], ADD)
+            nc.gpsimd.tensor_tensor(ctx[:], prods[0, k][:], prods[1, k][:], ADD)
             ctxs.append(ctx)
 
         inverse_den = held.tile([P, PAIRS], F32, name="inverse_den")
         nc.vector.reciprocal(inverse_den[:], den_psum[:])
 
-        pooled_psums = [psum.tile([P, PAIRS], F32, name=f"pooled_psum{b}") for b in range(FEATURE_BLOCKS)]
-        for k in range(TOKEN_BLOCKS):
-            for b in range(FEATURE_BLOCKS):
+        for b, queue in enumerate((nc.sync, nc.scalar)):
+            pooled_psum = psum.tile([P, PAIRS], F32, name=f"pooled_psum{b}")
+            for k in range(TOKEN_BLOCKS):
                 nc.tensor.matmul(
-                    pooled_psums[b][:], context_tile[:, k, b * P : (b + 1) * P], ctxs[k][:],
+                    pooled_psum[:], context_tile[:, k, b * P : (b + 1) * P], ctxs[k][:],
                     start=(k == 0), stop=(k == TOKEN_BLOCKS - 1),
                 )
-
-        for b, queue in enumerate((nc.sync, nc.scalar)):
             pooled = held.tile([P, PAIRS], F32, name=f"pooled{b}")
-            nc.vector.tensor_tensor(pooled[:], pooled_psums[b][:], inverse_den[:], MULT)
+            nc.vector.tensor_tensor(pooled[:], pooled_psum[:], inverse_den[:], MULT)
             queue.dma_start(out_blocks[b], pooled[:])

@@ -25,16 +25,20 @@ def tile_remodel_mention_kernel(tc, x, tail, context, offs, out):
         offsets = held.tile([P, PAIRS // 16], U16, name="offsets")
         nc.sync.dma_start(offsets[:], offs)
         tail_tiles, windows = [], {}
+        load_queues = (nc.scalar, nc.sync)
+        loads_started = 0
         for h in range(HEADS):
             tail_tile = held.tile([P, TOKEN_BLOCKS, PAIRS], F32, name=f"tail{h}")
-            nc.scalar.dma_start(tail_tile[:], tail_heads[h])
+            load_queues[loads_started % 2].dma_start(tail_tile[:], tail_heads[h])
+            loads_started += 1
             tail_tiles.append(tail_tile)
             for k in range(TOKEN_BLOCKS):
                 window = held.tile([P, ENTITIES], F32, name=f"window{h}{k}")
-                nc.scalar.dma_start(window[:], x_blocks[h, k])
+                load_queues[loads_started % 2].dma_start(window[:], x_blocks[h, k])
+                loads_started += 1
                 windows[h, k] = window
         context_tile = held.tile([P, TOKEN_BLOCKS, FEATURES], BF16, name="context_tile")
-        nc.scalar.dma_start(context_tile[:], context_rows)
+        load_queues[(loads_started - 1) % 2].dma_start(context_tile[:], context_rows)
 
         ones = held.tile([P, P], F32, name="ones")
         nc.vector.memset(ones[:], 1.0)

@@ -7,7 +7,7 @@ FEATURE_BLOCKS = FEATURES // P
 FLOPS = 2 * TOKENS * FEATURES * PAIRS
 
 F32, BF16, U16 = mybir.dt.float32, mybir.dt.bfloat16, mybir.dt.uint16
-MULT, ADD = mybir.AluOpType.mult, mybir.AluOpType.add
+MULT = mybir.AluOpType.mult
 
 
 def tile_remodel_mention_kernel(tc, x, tail, context, offs, out):
@@ -44,33 +44,27 @@ def tile_remodel_mention_kernel(tc, x, tail, context, offs, out):
         nc.vector.memset(ones[:], 1.0)
 
         den_psum = psum.tile([P, PAIRS], F32, name="den_psum")
-        prods = {}
+        pooled_psums = [psum.tile([P, PAIRS], F32, name=f"pooled_psum{b}") for b in range(FEATURE_BLOCKS)]
+
         for h in range(HEADS):
             for k in range(TOKEN_BLOCKS):
+                first = h == 0 and k == 0
+                last = h == HEADS - 1 and k == TOKEN_BLOCKS - 1
                 prod = held.tile([P, PAIRS], F32, name=f"prod{h}{k}")
                 nc.vector.tensor_tensor(prod[:], windows[h, k][:].indirect(offsets[:]), tail_tiles[h][:, k, :], MULT)
-                nc.tensor.matmul(
-                    den_psum[:], ones[:], prod[:],
-                    start=(h == 0 and k == 0), stop=(h == HEADS - 1 and k == TOKEN_BLOCKS - 1),
-                )
-                prods[h, k] = prod
-
-        ctxs = []
-        for k in range(TOKEN_BLOCKS):
-            ctx = held.tile([P, PAIRS], BF16, name=f"ctx{k}")
-            nc.gpsimd.tensor_tensor(ctx[:], prods[0, k][:], prods[1, k][:], ADD)
-            ctxs.append(ctx)
+                nc.tensor.matmul(den_psum[:], ones[:], prod[:], start=first, stop=last)
+                rounded = held.tile([P, PAIRS], BF16, name=f"rounded{h}{k}")
+                nc.scalar.copy(rounded[:], prod[:])
+                for b in range(FEATURE_BLOCKS):
+                    nc.tensor.matmul(
+                        pooled_psums[b][:], context_tile[:, k, b * P : (b + 1) * P], rounded[:],
+                        start=first, stop=last,
+                    )
 
         inverse_den = held.tile([P, PAIRS], F32, name="inverse_den")
         nc.vector.reciprocal(inverse_den[:], den_psum[:])
 
         for b, queue in enumerate((nc.sync, nc.scalar)):
-            pooled_psum = psum.tile([P, PAIRS], F32, name=f"pooled_psum{b}")
-            for k in range(TOKEN_BLOCKS):
-                nc.tensor.matmul(
-                    pooled_psum[:], context_tile[:, k, b * P : (b + 1) * P], ctxs[k][:],
-                    start=(k == 0), stop=(k == TOKEN_BLOCKS - 1),
-                )
             pooled = held.tile([P, PAIRS], F32, name=f"pooled{b}")
-            nc.vector.tensor_tensor(pooled[:], pooled_psum[:], inverse_den[:], MULT)
+            nc.vector.tensor_tensor(pooled[:], pooled_psums[b][:], inverse_den[:], MULT)
             queue.dma_start(out_blocks[b], pooled[:])

@@ -7,7 +7,7 @@ FEATURE_BLOCKS = FEATURES // P
 FLOPS = 2 * TOKENS * FEATURES * PAIRS
 
 F32, BF16, U16 = mybir.dt.float32, mybir.dt.bfloat16, mybir.dt.uint16
-MULT = mybir.AluOpType.mult
+MULT, ADD = mybir.AluOpType.mult, mybir.AluOpType.add
 
 
 def tile_remodel_mention_kernel(tc, x, tail, context, offs, out):
@@ -46,25 +46,41 @@ def tile_remodel_mention_kernel(tc, x, tail, context, offs, out):
         den_psum = psum.tile([P, PAIRS], F32, name="den_psum")
         pooled_psums = [psum.tile([P, PAIRS], F32, name=f"pooled_psum{b}") for b in range(FEATURE_BLOCKS)]
 
+        last_k = TOKEN_BLOCKS - 1
+        prods, pooling_inputs = {}, []
         for h in range(HEADS):
             for k in range(TOKEN_BLOCKS):
-                first = h == 0 and k == 0
-                last = h == HEADS - 1 and k == TOKEN_BLOCKS - 1
                 prod = held.tile([P, PAIRS], F32, name=f"prod{h}{k}")
                 nc.vector.tensor_tensor(prod[:], windows[h, k][:].indirect(offsets[:]), tail_tiles[h][:, k, :], MULT)
-                nc.tensor.matmul(den_psum[:], ones[:], prod[:], start=first, stop=last)
-                rounded = held.tile([P, PAIRS], BF16, name=f"rounded{h}{k}")
-                nc.scalar.copy(rounded[:], prod[:])
-                for b in range(FEATURE_BLOCKS):
-                    nc.tensor.matmul(
-                        pooled_psums[b][:], context_tile[:, k, b * P : (b + 1) * P], rounded[:],
-                        start=first, stop=last,
-                    )
+                nc.tensor.matmul(
+                    den_psum[:], ones[:], prod[:],
+                    start=h == 0 and k == 0, stop=h == HEADS - 1 and k == last_k,
+                )
+                prods[h, k] = prod
+                if k == last_k:
+                    rounded = held.tile([P, PAIRS], BF16, name=f"rounded{h}")
+                    nc.scalar.copy(rounded[:], prod[:])
+                    pooling_inputs.append((k, rounded))
+                elif h == HEADS - 1:
+                    ctx = held.tile([P, PAIRS], BF16, name=f"ctx{k}")
+                    nc.gpsimd.tensor_tensor(ctx[:], prods[0, k][:], prod[:], ADD)
+                    pooling_inputs.append((k, ctx))
 
-        inverse_den = held.tile([P, PAIRS], F32, name="inverse_den")
-        nc.vector.reciprocal(inverse_den[:], den_psum[:])
+        pooling_order = pooling_inputs[::-1]
+        for i, (k, weighted) in enumerate(pooling_order):
+            for b in range(FEATURE_BLOCKS):
+                nc.tensor.matmul(
+                    pooled_psums[b][:], context_tile[:, k, b * P : (b + 1) * P], weighted[:],
+                    start=i == 0, stop=i == len(pooling_order) - 1,
+                )
 
+        halves = (slice(0, PAIRS // 2), slice(PAIRS // 2, PAIRS))
+        inverse_den = [held.tile([P, PAIRS // 2], F32, name=f"inverse_den{i}") for i in range(2)]
+        for i, half in enumerate(halves):
+            nc.vector.reciprocal(inverse_den[i][:], den_psum[:, half])
+        pooled = [held.tile([P, PAIRS], F32, name=f"pooled{b}") for b in range(FEATURE_BLOCKS)]
+        for i, half in enumerate(halves):
+            for b in range(FEATURE_BLOCKS):
+                nc.vector.tensor_tensor(pooled[b][:, half], pooled_psums[b][:, half], inverse_den[i][:], MULT)
         for b, queue in enumerate((nc.sync, nc.scalar)):
-            pooled = held.tile([P, PAIRS], F32, name=f"pooled{b}")
-            nc.vector.tensor_tensor(pooled[:], pooled_psums[b][:], inverse_den[:], MULT)
-            queue.dma_start(out_blocks[b], pooled[:])
+            queue.dma_start(out_blocks[b], pooled[b][:])

@@ -23,7 +23,6 @@ def tile_remodel_mention_kernel(tc, x, tail, context, offs, out):
         tc.psum_pool(name="psum", bufs=1) as psum,
     ):
         offsets = held.tile([P, PAIRS // 16], U16, name="offsets")
-        nc.sync.dma_start(offsets[:], offs)
         tail_tiles, windows = [], {}
         load_queues = (nc.scalar, nc.sync)
         loads_started = 0
@@ -36,6 +35,8 @@ def tile_remodel_mention_kernel(tc, x, tail, context, offs, out):
                 window = held.tile([P, ENTITIES], F32, name=f"window{h}{k}")
                 load_queues[loads_started % 2].dma_start(window[:], x_blocks[h, k])
                 loads_started += 1
+                if h == 0 and k == 0:
+                    nc.sync.dma_start(offsets[:], offs)
                 windows[h, k] = window
         context_tile = held.tile([P, TOKEN_BLOCKS, FEATURES], BF16, name="context_tile")
         load_queues[(loads_started - 1) % 2].dma_start(context_tile[:], context_rows)

@@ -58,8 +58,8 @@ def tile_remodel_mention_kernel(tc, x, tail, context, offs, out):
                     start=h == 0 and k == 0, stop=h == HEADS - 1 and k == last_k,
                 )
                 prods[h, k] = prod
-                if k == last_k:
-                    rounded = held.tile([P, PAIRS], BF16, name=f"rounded{h}")
+                if k >= TOKEN_BLOCKS // 2:
+                    rounded = held.tile([P, PAIRS], BF16, name=f"rounded{h}{k}")
                     nc.scalar.copy(rounded[:], prod[:])
                     pooling_inputs.append((k, rounded))
                 elif h == HEADS - 1:

import concourse.mybir as mybir

HEADS, TOKENS, ENTITIES, PAIRS, FEATURES = 2, 512, 384, 128, 256
P = 128
TOKEN_BLOCKS = TOKENS // P
FEATURE_BLOCKS = FEATURES // P
FLOPS = 2 * TOKENS * FEATURES * PAIRS

F32, BF16, U16 = mybir.dt.float32, mybir.dt.bfloat16, mybir.dt.uint16
MULT, ADD = mybir.AluOpType.mult, mybir.AluOpType.add


def tile_remodel_mention_kernel(tc, x, tail, context, offs, out):
    nc = tc.nc

    x_blocks = x.rearrange("(h p k) s -> h k p s", h=HEADS, k=TOKEN_BLOCKS)
    tail_heads = tail.rearrange("(h p k) n -> h p k n", h=HEADS, k=TOKEN_BLOCKS)
    context_rows = context.rearrange("(p k) d -> p k d", k=TOKEN_BLOCKS)
    out_blocks = out.rearrange("(b p) n -> b p n", p=P)

    with (
        tc.tile_pool(name="held", bufs=1) as held,
        tc.psum_pool(name="psum", bufs=1) as psum,
    ):
        offsets = held.tile([P, PAIRS // 16], U16, name="offsets")
        tail_tiles, windows = [], {}
        load_queues = (nc.scalar, nc.sync)
        loads_started = 0
        for h in range(HEADS):
            tail_tile = held.tile([P, TOKEN_BLOCKS, PAIRS], F32, name=f"tail{h}")
            load_queues[loads_started % 2].dma_start(tail_tile[:], tail_heads[h])
            loads_started += 1
            tail_tiles.append(tail_tile)
            for k in range(TOKEN_BLOCKS):
                window = held.tile([P, ENTITIES], F32, name=f"window{h}{k}")
                load_queues[loads_started % 2].dma_start(window[:], x_blocks[h, k])
                loads_started += 1
                if h == 0 and k == 0:
                    nc.sync.dma_start(offsets[:], offs)
                windows[h, k] = window
        context_tile = held.tile([P, TOKEN_BLOCKS, FEATURES], BF16, name="context_tile")
        load_queues[(loads_started - 1) % 2].dma_start(context_tile[:], context_rows)

        ones = held.tile([P, P], F32, name="ones")
        nc.vector.memset(ones[:], 1.0)

        den_psum = psum.tile([P, PAIRS], F32, name="den_psum")
        pooled_psums = [psum.tile([P, PAIRS], F32, name=f"pooled_psum{b}") for b in range(FEATURE_BLOCKS)]

        last_k = TOKEN_BLOCKS - 1
        prods, pooling_inputs = {}, []
        for h in range(HEADS):
            for k in range(TOKEN_BLOCKS):
                prod = held.tile([P, PAIRS], F32, name=f"prod{h}{k}")
                nc.vector.tensor_tensor(prod[:], windows[h, k][:].indirect(offsets[:]), tail_tiles[h][:, k, :], MULT)
                nc.tensor.matmul(
                    den_psum[:], ones[:], prod[:],
                    start=h == 0 and k == 0, stop=h == HEADS - 1 and k == last_k,
                )
                prods[h, k] = prod
                if k >= TOKEN_BLOCKS // 2:
                    rounded = held.tile([P, PAIRS], BF16, name=f"rounded{h}{k}")
                    nc.scalar.copy(rounded[:], prod[:])
                    pooling_inputs.append((k, rounded))
                elif h == HEADS - 1:
                    ctx = held.tile([P, PAIRS], BF16, name=f"ctx{k}")
                    nc.gpsimd.tensor_tensor(ctx[:], prods[0, k][:], prod[:], ADD)
                    pooling_inputs.append((k, ctx))

        pooling_order = pooling_inputs[::-1]
        for i, (k, weighted) in enumerate(pooling_order):
            for b in range(FEATURE_BLOCKS):
                nc.tensor.matmul(
                    pooled_psums[b][:], context_tile[:, k, b * P : (b + 1) * P], weighted[:],
                    start=i == 0, stop=i == len(pooling_order) - 1,
                )

        halves = (slice(0, PAIRS // 2), slice(PAIRS // 2, PAIRS))
        inverse_den = [held.tile([P, PAIRS // 2], F32, name=f"inverse_den{i}") for i in range(2)]
        for i, half in enumerate(halves):
            nc.vector.reciprocal(inverse_den[i][:], den_psum[:, half])
        pooled = [held.tile([P, PAIRS], F32, name=f"pooled{b}") for b in range(FEATURE_BLOCKS)]
        for i, half in enumerate(halves):
            for b in range(FEATURE_BLOCKS):
                nc.vector.tensor_tensor(pooled[b][:, half], pooled_psums[b][:, half], inverse_den[i][:], MULT)
        for b, queue in enumerate((nc.sync, nc.scalar)):
            queue.dma_start(out_blocks[b], pooled[b][:])
